import numpy as np
import ml_dtypes


def mxq(x, axis, fmt="e4m3"):
    dtype, down = {"e4m3": (ml_dtypes.float8_e4m3fn, 7), "e5m2": (ml_dtypes.float8_e5m2, 14)}[fmt]
    v = np.moveaxis(np.asarray(x, np.float32).astype(ml_dtypes.bfloat16).astype(np.float64), axis, -1)
    blocks = v.reshape(v.shape[:-1] + (-1, 32))
    amax = np.abs(blocks).max(-1, keepdims=True)
    byte = np.maximum(np.where(amax > 0, np.frexp(amax)[1] - 1 + 127, 0) - down, 1)
    scale = np.exp2(byte - 127.0)
    codes = (blocks / scale).astype(np.float32).astype(dtype).astype(np.float64)
    return np.moveaxis((codes * scale).reshape(v.shape), -1, axis)


WIDE = False


def mx_kscale(k):
    if not WIDE:
        return np.ones(k)
    levels = np.array([10, -10, 5, -5, 0])
    a = np.random.permutation(np.resize(levels, k // 512 * 4)).reshape(k // 512, 4)
    idx = np.arange(k)
    return np.exp2(a[idx // 512, idx % 128 // 32])


BF16 = ml_dtypes.bfloat16


def bf(x):
    return np.asarray(x, np.float32).astype(BF16)


def f64(x):
    return np.asarray(x).astype(np.float64)


E2M1 = np.array([0.0, 0.5, 1.0, 1.5, 2.0, 3.0, 4.0, 6.0, -0.0, -0.5, -1.0, -1.5, -2.0, -3.0, -4.0, -6.0])


def pack_weight(w, fmt):
    k, n = w.shape
    w = f64(bf(w)).reshape(k // 32, 32, n)
    amax = np.abs(w).max(1)
    if fmt == "e4m3":
        byte = np.frexp(amax)[1] - 1 + 127 - 7
    else:
        mant, ex = np.frexp(amax / 6.0)
        byte = np.where(mant > 0.5, ex, ex - 1) + 127
    byte = np.clip(np.where(amax > 0, byte, 1), 1, 254)
    scaled = (w * np.exp2(127.0 - byte)[:, None, :]).reshape(k, n).astype(np.float32)
    by_word = np.ascontiguousarray(scaled.reshape(k // 512, 128, 4, n).transpose(0, 1, 3, 2))
    if fmt == "e4m3":
        words = by_word.astype(ml_dtypes.float8_e4m3fn).view(np.uint8)
    else:
        c = by_word.astype(ml_dtypes.float4_e2m1fn).view(np.uint8) & 0xF
        words = c[..., 0::2] | (c[..., 1::2] << 4)
    return np.ascontiguousarray(words), np.ascontiguousarray(byte.astype(np.uint8).reshape(k // 512, 16, n))


def unpack_weight(words, scales, fmt):
    g, p, n, _ = words.shape
    if fmt == "e4m3":
        vals = np.ascontiguousarray(words).view(ml_dtypes.float8_e4m3fn).astype(np.float64)
    else:
        nib = np.empty((g, p, n, 4), np.uint8)
        nib[..., 0::2] = words & 0xF
        nib[..., 1::2] = words >> 4
        vals = E2M1[nib]
    vals = vals * np.repeat(np.exp2(scales.astype(np.float64) - 127.0), 8, axis=1)[..., None]
    return vals.transpose(0, 1, 3, 2).reshape(g * 512, n)


B, D, C = 128, 64, 4096
EPS_SQRT = 1e-10
EPS_NORM = 1e-12
FMT = "e4m3"


def setup_inputs():
    s = mx_kscale(D * D)
    a = np.round(np.log2(np.array([s.max(), s.min()])) / 2)
    r = np.repeat(np.exp2(a - a.min()), D // 2)
    g = np.exp2(np.round(np.log2(np.mean(r ** 2))))
    feat = bf(np.random.standard_normal((B, D)) * r ** 2)
    w = np.random.standard_normal((C, D * D)) * g / np.outer(r, r).reshape(-1)
    words, scales = pack_weight(np.ascontiguousarray(w.T), FMT)
    b = bf(np.random.standard_normal(C) * 0.3)
    return {"feat": feat,
            "W_words": words,
            "W_scales": scales,
            "b": b}


def reference(feat, W_words, W_scales, b):
    feat = f64(feat)
    x = (feat[:, :, None] * feat[:, None, :]).reshape(feat.shape[0], -1)
    x = np.sign(x) * np.sqrt(np.abs(x) + EPS_SQRT)
    norm = np.maximum(np.linalg.norm(x, axis=1, keepdims=True), EPS_NORM)
    x = x / norm
    return (mxq(x, 1, "e4m3") @ unpack_weight(W_words, W_scales, FMT)) + f64(b)

@@ -1,0 +1,202 @@
+from contextlib import ExitStack
+
+import concourse.mybir as mybir
+from concourse.masks import make_identity
+
+F32 = mybir.dt.float32
+BF16 = mybir.dt.bfloat16
+I32 = mybir.dt.int32
+U32 = mybir.dt.uint32
+U8 = mybir.dt.uint8
+FP8X4 = mybir.dt.float8_e4m3fn_x4
+ACT = mybir.ActivationFunctionType
+ALU = mybir.AluOpType
+
+P = 128
+D = 64
+K = D * D
+C = 4096
+K_PASS = 512
+G = K // K_PASS
+N_TILE = 512
+BANKS = C // N_TILE
+EPS_SQRT = 1e-10
+EPS_NORM = 1e-12
+LAST_PIECES = 4
+PIECE = C // LAST_PIECES
+
+FLOPS = 2 * P * K * C
+
+
+def tile_bcnnresnet_w_kernel(tc, feat, W_words, W_scales, b, out):
+    nc = tc.nc
+    with ExitStack() as ctx:
+        keep = ctx.enter_context(tc.tile_pool(name="keep", bufs=1))
+        psum = ctx.enter_context(tc.psum_pool(name="psum", bufs=1))
+        ctx.enter_context(tc.manual_schedule())
+
+        feat_sb = keep.tile([P, D], BF16, name="feat_sb")
+        w_full = [keep.tile([P, C], U32, name="w%d" % g, align_bytes=64) for g in range(G - 1)]
+        w_last = [keep.tile([P, PIECE], U32, name="wl%d" % i, align_bytes=64) for i in range(LAST_PIECES)]
+        planes = [keep.tile([P, C], U8, name="planes%d" % a, align_bytes=64) for a in range(2)]
+        bpad = keep.tile([P, N_TILE], BF16, name="bpad")
+        ident = keep.tile([P, P], BF16, name="ident")
+        bias_sb = keep.tile([P, C], BF16, name="bias_sb")
+        out_sb = keep.tile([P, C], F32, name="out_sb")
+        mag = keep.tile([P, D], F32, name="mag")
+        sgn = keep.tile([P, D], BF16, name="sgn")
+        junk = keep.tile([P, D], BF16, name="junk")
+        sum_mag = keep.tile([P, 1], F32, name="sum_mag")
+        nnz = keep.tile([P, 1], F32, name="nnz")
+        t1 = keep.tile([P, 1], F32, name="t1")
+        t2 = keep.tile([P, 1], F32, name="t2")
+        n2 = keep.tile([P, 1], F32, name="n2")
+        inv2 = keep.tile([P, 1], F32, name="inv2")
+        e2 = keep.tile([P, 1], F32, name="e2")
+        q = keep.tile([P, K], F32, name="q")
+        x = keep.tile([P, K], BF16, name="x")
+        sg = keep.tile([P, K], BF16, name="sg")
+        grouped = keep.tile([P, K], BF16, name="grouped", align_bytes=64)
+        x_codes = keep.tile([P, G * P], U32, name="x_codes", align_bytes=64)
+        x_scales = keep.tile([P, G * P], U8, name="x_scales", align_bytes=64)
+
+        def w_src(g, c0, c1):
+            return W_words[g][:, c0:c1, :].rearrange("p n t -> p (n t)").bitcast(I32)
+
+        nc.vector.memset(bpad[:], 0.0)
+        for a in range(2):
+            nc.vector.memset(planes[a][:].bitcast(I32), 0)
+        make_identity(nc, ident[:])
+
+        nc.sync.dma_start(out=feat_sb[:], in_=feat)
+        nc.scalar.dma_start(out=bpad[0:BANKS, :], in_=b.rearrange("(r c) -> r c", r=BANKS))
+        nc.sync.dma_start(out=w_full[0][:].bitcast(I32), in_=w_src(0, 0, C))
+        for a in range(2):
+            for quad in range(4):
+                nc.sync.dma_start(
+                    out=planes[a][32 * quad : 32 * quad + 16, :].bitcast(I32),
+                    in_=W_scales[4 * a : 4 * a + 4, 4 * quad : 4 * quad + 4, :].bitcast(I32),
+                )
+        for g in range(1, G - 1):
+            nc.sync.dma_start(out=w_full[g][:].bitcast(I32), in_=w_src(g, 0, C))
+        for i in range(LAST_PIECES):
+            nc.sync.dma_start(out=w_last[i][:].bitcast(I32), in_=w_src(G - 1, i * PIECE, (i + 1) * PIECE))
+
+        bias_ps = []
+        for h in range(4):
+            bp = psum.tile([P, 2 * N_TILE], BF16, name="bias_ps%d" % h, tag="bk%d" % (4 + h))
+            bias_ps.append(bp)
+            for u in range(2):
+                j = 2 * h + u
+                nc.tensor.matmul(
+                    out=bp[:, u * N_TILE : (u + 1) * N_TILE],
+                    lhsT=ident[:, j : j + 1].to_broadcast([P, P]),
+                    rhs=bpad[:],
+                    start=True,
+                    stop=True,
+                )
+
+        def bias_copy(h):
+            nc.scalar.copy(out=bias_sb[:, 2 * h * N_TILE : 2 * (h + 1) * N_TILE], in_=bias_ps[h][:])
+
+        nc.scalar.activation(out=mag[:], in_=feat_sb[:], func=ACT.Abs, accum_out=sum_mag[:])
+        nc.scalar.activation(out=sgn[:], in_=feat_sb[:], func=ACT.Sign)
+        nc.scalar.activation(out=junk[:], in_=sgn[:], func=ACT.Abs, accum_out=nnz[:])
+        nc.vector.tensor_tensor(out=t1[:], in0=sum_mag[:], in1=sum_mag[:], op=ALU.mult)
+        nc.vector.tensor_scalar(out=t2[:], in0=nnz[:], scalar1=nnz[:, 0:1], scalar2=EPS_SQRT, op0=ALU.mult, op1=ALU.mult)
+        nc.vector.tensor_tensor(out=n2[:], in0=t1[:], in1=t2[:], op=ALU.add)
+        nc.vector.tensor_scalar_max(out=n2[:], in0=n2[:], scalar1=EPS_NORM * EPS_NORM)
+        nc.vector.reciprocal(out=inv2[:], in_=n2[:])
+        nc.vector.tensor_scalar_mul(out=e2[:], in0=inv2[:], scalar1=EPS_SQRT)
+
+        def blk(g):
+            return slice(g * K_PASS, (g + 1) * K_PASS)
+
+        def rows(v, g):
+            return v[:, 8 * g : 8 * g + 8].unsqueeze(1).unsqueeze(3).to_broadcast([P, 4, 8, 16])
+
+        def cols(v):
+            return v[:].rearrange("n (j t) -> n t j", t=4).unsqueeze(2).to_broadcast([P, 4, 8, 16])
+
+        def split(ap):
+            return ap.rearrange("n (t i j) -> n t i j", t=4, i=8)
+
+        def outer(g):
+            nc.vector.tensor_tensor(out=split(q[:, blk(g)]), in0=rows(mag, g), in1=cols(mag), op=ALU.mult)
+
+        def root(g):
+            nc.scalar.activation(out=x[:, blk(g)], in_=q[:, blk(g)], func=ACT.Sqrt, bias=e2[:, 0:1], scale=inv2[:, 0:1])
+
+        def signs(g):
+            nc.vector.tensor_tensor(out=split(sg[:, blk(g)]), in0=rows(sgn, g), in1=cols(sgn), op=ALU.mult)
+
+        def apply_sign(g):
+            nc.vector.tensor_tensor(out=x[:, blk(g)], in0=x[:, blk(g)], in1=sg[:, blk(g)], op=ALU.mult)
+
+        xt = [psum.tile([P, 2, 4, P], BF16, name="xt%d" % h, tag="bk%d" % h) for h in range(4)]
+
+        def flip(g):
+            for t in range(4):
+                c0 = g * K_PASS + t * P
+                nc.tensor.transpose(xt[g // 2][:, g % 2, t, :], x[:, c0 : c0 + P], ident[:])
+
+        def regroup(h):
+            nc.scalar.copy(
+                out=grouped[:, 2 * h * K_PASS : 2 * (h + 1) * K_PASS].rearrange("p (g n t) -> p g n t", g=2, t=4),
+                in_=xt[h][:].rearrange("p g t n -> p g n t"),
+            )
+
+        def quantise(h):
+            nc.vector.quantize_mx(
+                out=x_codes[:, 2 * h * P : 2 * (h + 1) * P].bitcast(FP8X4),
+                scales=x_scales[:, 2 * h * P : 2 * (h + 1) * P],
+                in_=grouped[:, 2 * h * K_PASS : 2 * (h + 1) * K_PASS],
+            )
+
+        for step in range(G + 3):
+            if step < G:
+                outer(step)
+                root(step)
+                signs(step)
+            if step in (3, 5):
+                bias_copy(step - 3)
+                bias_copy(step - 2)
+            ga = step - 1
+            if 0 <= ga < G:
+                apply_sign(ga)
+                flip(ga)
+                if ga % 2 == 1:
+                    regroup(ga // 2)
+            gq = step - 2
+            if 0 <= gq < G and gq % 2 == 1:
+                quantise(gq // 2)
+
+        acc = [psum.tile([P, N_TILE], F32, name="acc%d" % j, tag="bk%d" % j) for j in range(BANKS)]
+
+        def mx_pass(g, j):
+            if g < G - 1:
+                words = w_full[g][:, j * N_TILE : (j + 1) * N_TILE]
+            else:
+                per = PIECE // N_TILE
+                words = w_last[j // per][:, (j % per) * N_TILE : (j % per + 1) * N_TILE]
+            nc.tensor.matmul_mx(
+                out=acc[j][:],
+                lhsT=x_codes[:, g * P : (g + 1) * P].bitcast(FP8X4),
+                lhsT_scale=x_scales[:, g * P : (g + 1) * P],
+                rhs=words.bitcast(FP8X4),
+                rhs_scale=planes[g // 4][4 * (g % 4) : P, j * N_TILE : (j + 1) * N_TILE],
+                start=(g == 0),
+                stop=(g == G - 1),
+            )
+
+        for g in range(G - 1):
+            for j in range(BANKS):
+                mx_pass(g, j)
+        per = PIECE // N_TILE
+        for i in range(LAST_PIECES):
+            for j in range(i * per, (i + 1) * per):
+                mx_pass(G - 1, j)
+                cs = slice(j * N_TILE, (j + 1) * N_TILE)
+                nc.vector.tensor_tensor(out=out_sb[:, cs], in0=acc[j][:], in1=bias_sb[:, cs], op=ALU.add)
+            ps = slice(i * PIECE, (i + 1) * PIECE)
+            nc.sync.dma_start(out=out[:, ps], in_=out_sb[:, ps])

@@ -22,8 +22,10 @@ N_TILE = 512
 BANKS = C // N_TILE
 EPS_SQRT = 1e-10
 EPS_NORM = 1e-12
-LAST_PIECES = 4
-PIECE = C // LAST_PIECES
+BANKS_1 = 6
+C1 = BANKS_1 * N_TILE
+C2 = C - C1
+QUADS = (0, 1, 2, 3)
 
 FLOPS = 2 * P * K * C
 
@@ -36,8 +38,9 @@ def tile_bcnnresnet_w_kernel(tc, feat, W_words, W_scales, b, out):
         ctx.enter_context(tc.manual_schedule())
 
         feat_sb = keep.tile([P, D], BF16, name="feat_sb")
-        w_full = [keep.tile([P, C], U32, name="w%d" % g, align_bytes=64) for g in range(G - 1)]
-        w_last = [keep.tile([P, PIECE], U32, name="wl%d" % i, align_bytes=64) for i in range(LAST_PIECES)]
+        w1 = [keep.tile([P, C1], U32, name="w1_%d" % g, align_bytes=64) for g in range(G)]
+        w2 = [keep.tile([P, C2], U32, name="w2_%d" % g, align_bytes=64) for g in range(G - 1)]
+        w2_last = [keep.tile([P, N_TILE], U32, name="w2l_%d" % i, align_bytes=64) for i in range(2)]
         planes = [keep.tile([P, C], U8, name="planes%d" % a, align_bytes=64) for a in range(2)]
         bpad = keep.tile([P, N_TILE], BF16, name="bpad")
         ident = keep.tile([P, P], BF16, name="ident")
@@ -70,34 +73,19 @@ def tile_bcnnresnet_w_kernel(tc, feat, W_words, W_scales, b, out):
 
         nc.sync.dma_start(out=feat_sb[:], in_=feat)
         nc.scalar.dma_start(out=bpad[0:BANKS, :], in_=b.rearrange("(r c) -> r c", r=BANKS))
-        nc.sync.dma_start(out=w_full[0][:].bitcast(I32), in_=w_src(0, 0, C))
+        nc.sync.dma_start(out=w1[0][:].bitcast(I32), in_=w_src(0, 0, C1))
         for a in range(2):
-            for quad in range(4):
+            for quad in QUADS:
                 nc.sync.dma_start(
                     out=planes[a][32 * quad : 32 * quad + 16, :].bitcast(I32),
                     in_=W_scales[4 * a : 4 * a + 4, 4 * quad : 4 * quad + 4, :].bitcast(I32),
                 )
-        for g in range(1, G - 1):
-            nc.sync.dma_start(out=w_full[g][:].bitcast(I32), in_=w_src(g, 0, C))
-        for i in range(LAST_PIECES):
-            nc.sync.dma_start(out=w_last[i][:].bitcast(I32), in_=w_src(G - 1, i * PIECE, (i + 1) * PIECE))
-
-        bias_ps = []
-        for h in range(4):
-            bp = psum.tile([P, 2 * N_TILE], BF16, name="bias_ps%d" % h, tag="bk%d" % (4 + h))
-            bias_ps.append(bp)
-            for u in range(2):
-                j = 2 * h + u
-                nc.tensor.matmul(
-                    out=bp[:, u * N_TILE : (u + 1) * N_TILE],
-                    lhsT=ident[:, j : j + 1].to_broadcast([P, P]),
-                    rhs=bpad[:],
-                    start=True,
-                    stop=True,
-                )
-
-        def bias_copy(h):
-            nc.scalar.copy(out=bias_sb[:, 2 * h * N_TILE : 2 * (h + 1) * N_TILE], in_=bias_ps[h][:])
+        for g in range(1, G):
+            nc.sync.dma_start(out=w1[g][:].bitcast(I32), in_=w_src(g, 0, C1))
+        for g in range(G - 1):
+            nc.sync.dma_start(out=w2[g][:].bitcast(I32), in_=w_src(g, C1, C))
+        for i in range(2):
+            nc.sync.dma_start(out=w2_last[i][:].bitcast(I32), in_=w_src(G - 1, C1 + i * N_TILE, C1 + (i + 1) * N_TILE))
 
         nc.scalar.activation(out=mag[:], in_=feat_sb[:], func=ACT.Abs, accum_out=sum_mag[:])
         nc.scalar.activation(out=sgn[:], in_=feat_sb[:], func=ACT.Sign)
@@ -133,12 +121,15 @@ def tile_bcnnresnet_w_kernel(tc, feat, W_words, W_scales, b, out):
         def apply_sign(g):
             nc.vector.tensor_tensor(out=x[:, blk(g)], in0=x[:, blk(g)], in1=sg[:, blk(g)], op=ALU.mult)
 
-        xt = [psum.tile([P, 2, 4, P], BF16, name="xt%d" % h, tag="bk%d" % h) for h in range(4)]
+        xt = {}
 
         def flip(g):
+            h = g // 2
+            if g % 2 == 0:
+                xt[h] = psum.tile([P, 2, 4, P], BF16, name="xt%d" % h, tag="bk%d" % (BANKS_1 + h % 2))
             for t in range(4):
                 c0 = g * K_PASS + t * P
-                nc.tensor.transpose(xt[g // 2][:, g % 2, t, :], x[:, c0 : c0 + P], ident[:])
+                nc.tensor.transpose(xt[h][:, g % 2, t, :], x[:, c0 : c0 + P], ident[:])
 
         def regroup(h):
             nc.scalar.copy(
@@ -153,32 +144,17 @@ def tile_bcnnresnet_w_kernel(tc, feat, W_words, W_scales, b, out):
                 in_=grouped[:, 2 * h * K_PASS : 2 * (h + 1) * K_PASS],
             )
 
-        for step in range(G + 3):
-            if step < G:
-                outer(step)
-                root(step)
-                signs(step)
-            if step in (3, 5):
-                bias_copy(step - 3)
-                bias_copy(step - 2)
-            ga = step - 1
-            if 0 <= ga < G:
-                apply_sign(ga)
-                flip(ga)
-                if ga % 2 == 1:
-                    regroup(ga // 2)
-            gq = step - 2
-            if 0 <= gq < G and gq % 2 == 1:
-                quantise(gq // 2)
-
-        acc = [psum.tile([P, N_TILE], F32, name="acc%d" % j, tag="bk%d" % j) for j in range(BANKS)]
+        acc = {}
+        for j in range(BANKS_1):
+            acc[j] = psum.tile([P, N_TILE], F32, name="acc%d" % j, tag="bk%d" % j)
 
         def mx_pass(g, j):
-            if g < G - 1:
-                words = w_full[g][:, j * N_TILE : (j + 1) * N_TILE]
+            if j < BANKS_1:
+                words = w1[g][:, j * N_TILE : (j + 1) * N_TILE]
+            elif g < G - 1:
+                words = w2[g][:, (j - BANKS_1) * N_TILE : (j - BANKS_1 + 1) * N_TILE]
             else:
-                per = PIECE // N_TILE
-                words = w_last[j // per][:, (j % per) * N_TILE : (j % per + 1) * N_TILE]
+                words = w2_last[j - BANKS_1][:]
             nc.tensor.matmul_mx(
                 out=acc[j][:],
                 lhsT=x_codes[:, g * P : (g + 1) * P].bitcast(FP8X4),
@@ -189,14 +165,72 @@ def tile_bcnnresnet_w_kernel(tc, feat, W_words, W_scales, b, out):
                 stop=(g == G - 1),
             )
 
-        for g in range(G - 1):
-            for j in range(BANKS):
+        def block1(g):
+            for j in range(BANKS_1):
                 mx_pass(g, j)
-        per = PIECE // N_TILE
-        for i in range(LAST_PIECES):
-            for j in range(i * per, (i + 1) * per):
-                mx_pass(G - 1, j)
-                cs = slice(j * N_TILE, (j + 1) * N_TILE)
-                nc.vector.tensor_tensor(out=out_sb[:, cs], in0=acc[j][:], in1=bias_sb[:, cs], op=ALU.add)
-            ps = slice(i * PIECE, (i + 1) * PIECE)
-            nc.sync.dma_start(out=out[:, ps], in_=out_sb[:, ps])
+
+        def add_bias(j):
+            cs = slice(j * N_TILE, (j + 1) * N_TILE)
+            nc.vector.tensor_tensor(out=out_sb[:, cs], in0=acc[j][:], in1=bias_sb[:, cs], op=ALU.add)
+
+        def store(j0, j1):
+            cs = slice(j0 * N_TILE, j1 * N_TILE)
+            nc.sync.dma_start(out=out[:, cs], in_=out_sb[:, cs])
+
+        def bias_round(r):
+            for u in range(2):
+                h = 2 * r + u
+                bp = psum.tile([P, 2 * N_TILE], BF16, name="bias_ps%d" % h, tag="bk%d" % (BANKS_1 + u))
+                for v in range(2):
+                    j = 2 * h + v
+                    nc.tensor.matmul(
+                        out=bp[:, v * N_TILE : (v + 1) * N_TILE],
+                        lhsT=ident[:, j : j + 1].to_broadcast([P, P]),
+                        rhs=bpad[:],
+                        start=True,
+                        stop=True,
+                    )
+                nc.scalar.copy(out=bias_sb[:, 2 * h * N_TILE : 2 * (h + 1) * N_TILE], in_=bp[:])
+
+        for step in range(G + 2):
+            if step < G:
+                outer(step)
+                root(step)
+                signs(step)
+            ga = step - 1
+            if 0 <= ga < G:
+                apply_sign(ga)
+                flip(ga)
+                if ga % 2 == 1:
+                    regroup(ga // 2)
+            gq = step - 2
+            if 0 <= gq < G and gq % 2 == 1:
+                quantise(gq // 2)
+            if step == 4:
+                block1(0)
+                block1(1)
+            if step == 6:
+                block1(2)
+            if step == 8:
+                block1(3)
+
+        bias_round(0)
+        block1(4)
+        bias_round(1)
+        block1(5)
+        block1(6)
+        for j in range(BANKS_1):
+            mx_pass(G - 1, j)
+            add_bias(j)
+            if j % 2 == 1:
+                store(j - 1, j + 1)
+
+        for j in range(BANKS_1, BANKS):
+            acc[j] = psum.tile([P, N_TILE], F32, name="acc%d" % j, tag="bk%d" % j)
+        for g in range(G - 1):
+            for j in range(BANKS_1, BANKS):
+                mx_pass(g, j)
+        for j in range(BANKS_1, BANKS):
+            mx_pass(G - 1, j)
+            add_bias(j)
+            store(j, j + 1)

@@ -25,7 +25,7 @@ EPS_NORM = 1e-12
 BANKS_1 = 6
 C1 = BANKS_1 * N_TILE
 C2 = C - C1
-QUADS = (0, 1, 2, 3)
+QUADS = (0, 2, 1, 3)
 
 FLOPS = 2 * P * K * C
 
@@ -76,9 +76,9 @@ def tile_bcnnresnet_w_kernel(tc, feat, W_words, W_scales, b, out):
         nc.sync.dma_start(out=w1[0][:].bitcast(I32), in_=w_src(0, 0, C1))
         for a in range(2):
             for quad in QUADS:
-                nc.sync.dma_start(
-                    out=planes[a][32 * quad : 32 * quad + 16, :].bitcast(I32),
-                    in_=W_scales[4 * a : 4 * a + 4, 4 * quad : 4 * quad + 4, :].bitcast(I32),
+                nc.gpsimd.dma_start(
+                    out=planes[a][32 * quad : 32 * quad + 16, :].bitcast(F32),
+                    in_=W_scales[4 * a : 4 * a + 4, 4 * quad : 4 * quad + 4, :].bitcast(F32),
                 )
         for g in range(1, G):
             nc.sync.dma_start(out=w1[g][:].bitcast(I32), in_=w_src(g, 0, C1))

@@ -56,6 +56,7 @@ def tile_bcnnresnet_w_kernel(tc, feat, W_words, W_scales, b, out):
         n2 = keep.tile([P, 1], F32, name="n2")
         inv2 = keep.tile([P, 1], F32, name="inv2")
         e2 = keep.tile([P, 1], F32, name="e2")
+        spacer = keep.tile([P, 8], F32, name="spacer")
         q = keep.tile([P, K], F32, name="q")
         x = keep.tile([P, K], BF16, name="x")
         sg = keep.tile([P, K], BF16, name="sg")
@@ -79,6 +80,10 @@ def tile_bcnnresnet_w_kernel(tc, feat, W_words, W_scales, b, out):
                 nc.gpsimd.dma_start(
                     out=planes[a][32 * quad : 32 * quad + 16, :].bitcast(F32),
                     in_=W_scales[4 * a : 4 * a + 4, 4 * quad : 4 * quad + 4, :].bitcast(F32),
+                )
+                nc.gpsimd.dma_start(
+                    out=spacer[32 * quad + 16 : 32 * quad + 32, :],
+                    in_=W_scales[4 * a : 4 * a + 4, 4 * quad : 4 * quad + 4, 0:32].bitcast(F32),
                 )
         for g in range(1, G):
             nc.sync.dma_start(out=w1[g][:].bitcast(I32), in_=w_src(g, 0, C1))

from contextlib import ExitStack

import concourse.mybir as mybir
from concourse.masks import make_identity

F32 = mybir.dt.float32
BF16 = mybir.dt.bfloat16
I32 = mybir.dt.int32
U32 = mybir.dt.uint32
U8 = mybir.dt.uint8
FP8X4 = mybir.dt.float8_e4m3fn_x4
ACT = mybir.ActivationFunctionType
ALU = mybir.AluOpType

P = 128
D = 64
K = D * D
C = 4096
K_PASS = 512
G = K // K_PASS
N_TILE = 512
BANKS = C // N_TILE
EPS_SQRT = 1e-10
EPS_NORM = 1e-12
BANKS_1 = 6
C1 = BANKS_1 * N_TILE
C2 = C - C1
QUADS = (0, 2, 1, 3)

FLOPS = 2 * P * K * C


def tile_bcnnresnet_w_kernel(tc, feat, W_words, W_scales, b, out):
    nc = tc.nc
    with ExitStack() as ctx:
        keep = ctx.enter_context(tc.tile_pool(name="keep", bufs=1))
        psum = ctx.enter_context(tc.psum_pool(name="psum", bufs=1))
        ctx.enter_context(tc.manual_schedule())

        feat_sb = keep.tile([P, D], BF16, name="feat_sb")
        w1 = [keep.tile([P, C1], U32, name="w1_%d" % g, align_bytes=64) for g in range(G)]
        w2 = [keep.tile([P, C2], U32, name="w2_%d" % g, align_bytes=64) for g in range(G - 1)]
        w2_last = [keep.tile([P, N_TILE], U32, name="w2l_%d" % i, align_bytes=64) for i in range(2)]
        planes = [keep.tile([P, C], U8, name="planes%d" % a, align_bytes=64) for a in range(2)]
        bpad = keep.tile([P, N_TILE], BF16, name="bpad")
        ident = keep.tile([P, P], BF16, name="ident")
        bias_sb = keep.tile([P, C], BF16, name="bias_sb")
        out_sb = keep.tile([P, C], F32, name="out_sb")
        mag = keep.tile([P, D], F32, name="mag")
        sgn = keep.tile([P, D], BF16, name="sgn")
        junk = keep.tile([P, D], BF16, name="junk")
        sum_mag = keep.tile([P, 1], F32, name="sum_mag")
        nnz = keep.tile([P, 1], F32, name="nnz")
        t1 = keep.tile([P, 1], F32, name="t1")
        t2 = keep.tile([P, 1], F32, name="t2")
        n2 = keep.tile([P, 1], F32, name="n2")
        inv2 = keep.tile([P, 1], F32, name="inv2")
        e2 = keep.tile([P, 1], F32, name="e2")
        spacer = keep.tile([P, 8], F32, name="spacer")
        q = keep.tile([P, K], F32, name="q")
        x = keep.tile([P, K], BF16, name="x")
        sg = keep.tile([P, K], BF16, name="sg")
        grouped = keep.tile([P, K], BF16, name="grouped", align_bytes=64)
        x_codes = keep.tile([P, G * P], U32, name="x_codes", align_bytes=64)
        x_scales = keep.tile([P, G * P], U8, name="x_scales", align_bytes=64)

        def w_src(g, c0, c1):
            return W_words[g][:, c0:c1, :].rearrange("p n t -> p (n t)").bitcast(I32)

        nc.vector.memset(bpad[:], 0.0)
        for a in range(2):
            nc.vector.memset(planes[a][:].bitcast(I32), 0)
        make_identity(nc, ident[:])

        nc.sync.dma_start(out=feat_sb[:], in_=feat)
        nc.scalar.dma_start(out=bpad[0:BANKS, :], in_=b.rearrange("(r c) -> r c", r=BANKS))
        nc.sync.dma_start(out=w1[0][:].bitcast(I32), in_=w_src(0, 0, C1))
        for a in range(2):
            for quad in QUADS:
                nc.gpsimd.dma_start(
                    out=planes[a][32 * quad : 32 * quad + 16, :].bitcast(F32),
                    in_=W_scales[4 * a : 4 * a + 4, 4 * quad : 4 * quad + 4, :].bitcast(F32),
                )
                nc.gpsimd.dma_start(
                    out=spacer[32 * quad + 16 : 32 * quad + 32, :],
                    in_=W_scales[4 * a : 4 * a + 4, 4 * quad : 4 * quad + 4, 0:32].bitcast(F32),
                )
        for g in range(1, G):
            nc.sync.dma_start(out=w1[g][:].bitcast(I32), in_=w_src(g, 0, C1))
        for g in range(G - 1):
            nc.sync.dma_start(out=w2[g][:].bitcast(I32), in_=w_src(g, C1, C))
        for i in range(2):
            nc.sync.dma_start(out=w2_last[i][:].bitcast(I32), in_=w_src(G - 1, C1 + i * N_TILE, C1 + (i + 1) * N_TILE))

        nc.scalar.activation(out=mag[:], in_=feat_sb[:], func=ACT.Abs, accum_out=sum_mag[:])
        nc.scalar.activation(out=sgn[:], in_=feat_sb[:], func=ACT.Sign)
        nc.scalar.activation(out=junk[:], in_=sgn[:], func=ACT.Abs, accum_out=nnz[:])
        nc.vector.tensor_tensor(out=t1[:], in0=sum_mag[:], in1=sum_mag[:], op=ALU.mult)
        nc.vector.tensor_scalar(out=t2[:], in0=nnz[:], scalar1=nnz[:, 0:1], scalar2=EPS_SQRT, op0=ALU.mult, op1=ALU.mult)
        nc.vector.tensor_tensor(out=n2[:], in0=t1[:], in1=t2[:], op=ALU.add)
        nc.vector.tensor_scalar_max(out=n2[:], in0=n2[:], scalar1=EPS_NORM * EPS_NORM)
        nc.vector.reciprocal(out=inv2[:], in_=n2[:])
        nc.vector.tensor_scalar_mul(out=e2[:], in0=inv2[:], scalar1=EPS_SQRT)

        def blk(g):
            return slice(g * K_PASS, (g + 1) * K_PASS)

        def rows(v, g):
            return v[:, 8 * g : 8 * g + 8].unsqueeze(1).unsqueeze(3).to_broadcast([P, 4, 8, 16])

        def cols(v):
            return v[:].rearrange("n (j t) -> n t j", t=4).unsqueeze(2).to_broadcast([P, 4, 8, 16])

        def split(ap):
            return ap.rearrange("n (t i j) -> n t i j", t=4, i=8)

        def outer(g):
            nc.vector.tensor_tensor(out=split(q[:, blk(g)]), in0=rows(mag, g), in1=cols(mag), op=ALU.mult)

        def root(g):
            nc.scalar.activation(out=x[:, blk(g)], in_=q[:, blk(g)], func=ACT.Sqrt, bias=e2[:, 0:1], scale=inv2[:, 0:1])

        def signs(g):
            nc.vector.tensor_tensor(out=split(sg[:, blk(g)]), in0=rows(sgn, g), in1=cols(sgn), op=ALU.mult)

        def apply_sign(g):
            nc.vector.tensor_tensor(out=x[:, blk(g)], in0=x[:, blk(g)], in1=sg[:, blk(g)], op=ALU.mult)

        xt = {}

        def flip(g):
            h = g // 2
            if g % 2 == 0:
                xt[h] = psum.tile([P, 2, 4, P], BF16, name="xt%d" % h, tag="bk%d" % (BANKS_1 + h % 2))
            for t in range(4):
                c0 = g * K_PASS + t * P
                nc.tensor.transpose(xt[h][:, g % 2, t, :], x[:, c0 : c0 + P], ident[:])

        def regroup(h):
            nc.scalar.copy(
                out=grouped[:, 2 * h * K_PASS : 2 * (h + 1) * K_PASS].rearrange("p (g n t) -> p g n t", g=2, t=4),
                in_=xt[h][:].rearrange("p g t n -> p g n t"),
            )

        def quantise(h):
            nc.vector.quantize_mx(
                out=x_codes[:, 2 * h * P : 2 * (h + 1) * P].bitcast(FP8X4),
                scales=x_scales[:, 2 * h * P : 2 * (h + 1) * P],
                in_=grouped[:, 2 * h * K_PASS : 2 * (h + 1) * K_PASS],
            )

        acc = {}
        for j in range(BANKS_1):
            acc[j] = psum.tile([P, N_TILE], F32, name="acc%d" % j, tag="bk%d" % j)

        def mx_pass(g, j):
            if j < BANKS_1:
                words = w1[g][:, j * N_TILE : (j + 1) * N_TILE]
            elif g < G - 1:
                words = w2[g][:, (j - BANKS_1) * N_TILE : (j - BANKS_1 + 1) * N_TILE]
            else:
                words = w2_last[j - BANKS_1][:]
            nc.tensor.matmul_mx(
                out=acc[j][:],
                lhsT=x_codes[:, g * P : (g + 1) * P].bitcast(FP8X4),
                lhsT_scale=x_scales[:, g * P : (g + 1) * P],
                rhs=words.bitcast(FP8X4),
                rhs_scale=planes[g // 4][4 * (g % 4) : P, j * N_TILE : (j + 1) * N_TILE],
                start=(g == 0),
                stop=(g == G - 1),
            )

        def block1(g):
            for j in range(BANKS_1):
                mx_pass(g, j)

        def add_bias(j):
            cs = slice(j * N_TILE, (j + 1) * N_TILE)
            nc.vector.tensor_tensor(out=out_sb[:, cs], in0=acc[j][:], in1=bias_sb[:, cs], op=ALU.add)

        def store(j0, j1):
            cs = slice(j0 * N_TILE, j1 * N_TILE)
            nc.sync.dma_start(out=out[:, cs], in_=out_sb[:, cs])

        def bias_round(r):
            for u in range(2):
                h = 2 * r + u
                bp = psum.tile([P, 2 * N_TILE], BF16, name="bias_ps%d" % h, tag="bk%d" % (BANKS_1 + u))
                for v in range(2):
                    j = 2 * h + v
                    nc.tensor.matmul(
                        out=bp[:, v * N_TILE : (v + 1) * N_TILE],
                        lhsT=ident[:, j : j + 1].to_broadcast([P, P]),
                        rhs=bpad[:],
                        start=True,
                        stop=True,
                    )
                nc.scalar.copy(out=bias_sb[:, 2 * h * N_TILE : 2 * (h + 1) * N_TILE], in_=bp[:])

        for step in range(G + 2):
            if step < G:
                outer(step)
                root(step)
                signs(step)
            ga = step - 1
            if 0 <= ga < G:
                apply_sign(ga)
                flip(ga)
                if ga % 2 == 1:
                    regroup(ga // 2)
            gq = step - 2
            if 0 <= gq < G and gq % 2 == 1:
                quantise(gq // 2)
            if step == 4:
                block1(0)
                block1(1)
            if step == 6:
                block1(2)
            if step == 8:
                block1(3)

        bias_round(0)
        block1(4)
        bias_round(1)
        block1(5)
        block1(6)
        for j in range(BANKS_1):
            mx_pass(G - 1, j)
            add_bias(j)
            if j % 2 == 1:
                store(j - 1, j + 1)

        for j in range(BANKS_1, BANKS):
            acc[j] = psum.tile([P, N_TILE], F32, name="acc%d" % j, tag="bk%d" % j)
        for g in range(G - 1):
            for j in range(BANKS_1, BANKS):
                mx_pass(g, j)
        for j in range(BANKS_1, BANKS):
            mx_pass(G - 1, j)
            add_bias(j)
            store(j, j + 1)
